import numpy as np
import ml_dtypes

BF16 = ml_dtypes.bfloat16


def bf(x):
    return np.asarray(x, np.float32).astype(BF16)


def f32(x):
    return np.asarray(x, np.float32)


def f64(x):
    return np.asarray(x).astype(np.float64)


def striped(idx):
    return np.tile(idx.reshape(-1, 16).T, (8, 1))


C, S, F, B, T, N = 1024, 256, 64, 4, 256, 1024
TSTEP = 1.0


def setup_inputs():
    return {"x": f32(np.random.standard_normal((C, S))), "amp": f32(np.sqrt(2.0 / F) * np.random.standard_normal((C, F))), "freq": f32(np.random.uniform(0.05, 0.45, (1, F))), "offs": striped(np.concatenate([np.random.permutation(S) for _ in range(B)]))}


def reference(x, amp, freq, offs):
    idx = offs[:16].T.reshape(-1)
    th = 2.0 * np.pi * f64(freq)[0] * TSTEP
    p = (f64(amp) * np.cos(th)[None, :]).sum(axis=1, keepdims=True)
    q = (f64(amp) * np.sin(th)[None, :]).sum(axis=1, keepdims=True)
    ang = 2.0 * np.pi * (np.arange(N) % T) / T
    coef = p * np.cos(ang)[None, :] + q * np.sin(ang)[None, :]
    return f64(x)[:, idx] * coef

@@ -1,0 +1,105 @@
+import concourse.mybir as mybir
+from concourse.masks import make_identity
+
+F32 = mybir.dt.float32
+I32 = mybir.dt.int32
+U16 = mybir.dt.uint16
+ALU = mybir.AluOpType
+ACT = mybir.ActivationFunctionType
+
+P = 128
+C, S, F, N = 1024, 256, 64, 1024
+BLOCKS = C // P
+PAIRS = BLOCKS // 2
+PIECES = N // S
+QUARTER = S // 4
+
+TWO_PI = 6.283185
+
+FLOPS = 2 * C * F * S + C * N
+
+
+def fold(nc, out, turns):
+    nc.vector.scalar_tensor_tensor(out=out, in0=turns, scalar=0.5, in1=turns, op0=ALU.is_gt, op1=ALU.subtract)
+
+
+def tile_waveencoder_kernel(tc, x, amp, freq, offs, out):
+    nc = tc.nc
+    with (
+        tc.tile_pool(name="held", bufs=1) as held,
+        tc.tile_pool(name="products", bufs=8) as products,
+        tc.psum_pool(name="flipped", bufs=2) as flipped,
+        tc.psum_pool(name="sums", bufs=4) as sums,
+    ):
+        freq_col = held.tile([P, 1], F32, name="freq_col")
+        with nc.allow_non_contiguous_dma(reason="64 frequencies, one to a partition"):
+            nc.sync.dma_start(freq_col[0:F, :], freq.rearrange("o m -> m o"))
+            nc.scalar.dma_start(freq_col[F:P, :], freq.rearrange("o m -> m o"))
+        offsets = held.tile([P, N // 16], U16, name="offsets")
+        nc.sync.dma_start(offsets[:], offs)
+        amp_pairs = []
+        for j in range(PAIRS):
+            amp_pair = held.tile([P, 2, F], F32, name=f"amp_pair{j}")
+            nc.scalar.dma_start(amp_pair[:], amp[2 * j * P : (2 * j + 2) * P, :].rearrange("(b p) m -> p b m", p=P))
+            amp_pairs.append(amp_pair)
+        tables = []
+        for b in range(BLOCKS):
+            table = held.tile([P, S], F32, name=f"table{b}")
+            nc.sync.dma_start(table[:], x[b * P : (b + 1) * P, :])
+            tables.append(table)
+
+        identity = held.tile([P, P], F32, name="identity")
+        make_identity(nc, identity[:])
+        position = held.tile([P, S + QUARTER], F32, name="position")
+        nc.gpsimd.iota(position[:, 0 : S // 2], pattern=[[1, S // 2]], base=0, channel_multiplier=0,
+                       allow_small_or_imprecise_dtypes=True)
+        nc.gpsimd.iota(position[:, S // 2 :], pattern=[[1, S // 2 + QUARTER]], base=-(S // 2), channel_multiplier=0,
+                       allow_small_or_imprecise_dtypes=True)
+        sine = held.tile([P, S + QUARTER], F32, name="sine")
+        nc.scalar.activation(out=sine[:], in_=position[:], func=ACT.Sin, scale=TWO_PI / S)
+        sin_a = sine[:, 0:S]
+        cos_a = sine[:, QUARTER : QUARTER + S]
+        phase = held.tile([P, 2], F32, name="phase")
+        nc.vector.memset(phase[:, 0:1], 0.25)
+        nc.vector.memset(phase[:, 1:2], 0.0)
+        wave_diag = held.tile([P, 2 * S], F32, name="wave_diag")
+        nc.gpsimd.memset(wave_diag[0:F, S : 2 * S], 0.0)
+        nc.gpsimd.memset(wave_diag[F:P, 0:S], 0.0)
+
+        whole = held.tile([P, 1], I32, name="whole")
+        nc.vector.tensor_copy(whole[:], freq_col[:])
+        minus_turns = held.tile([P, 2], F32, name="minus_turns")
+        nc.vector.scalar_tensor_tensor(out=minus_turns[:], in0=whole[:, 0:1].to_broadcast([P, 2]), scalar=freq_col[:, 0:1],
+                                       in1=phase[:], op0=ALU.subtract, op1=ALU.subtract)
+        folded_once = held.tile([P, 2], F32, name="folded_once")
+        fold(nc, folded_once[:], minus_turns[:])
+        folded = held.tile([P, 2], F32, name="folded")
+        fold(nc, folded[:], folded_once[:])
+        cos_sin_th = held.tile([P, 2], F32, name="cos_sin_th")
+        nc.scalar.activation(out=cos_sin_th[:], in_=folded[:], func=ACT.Sin, scale=-TWO_PI)
+
+        cos_part = held.tile([P, S], F32, name="cos_part")
+        nc.vector.tensor_scalar(out=cos_part[:], in0=cos_a, scalar1=cos_sin_th[:, 0:1], scalar2=None, op0=ALU.mult)
+        for h in range(2):
+            rows = slice(h * F, (h + 1) * F)
+            nc.vector.scalar_tensor_tensor(out=wave_diag[rows, h * S : (h + 1) * S], in0=sin_a[rows, :],
+                                           scalar=cos_sin_th[rows, 1:2], in1=cos_part[rows, :],
+                                           op0=ALU.mult, op1=ALU.add)
+
+        for j in range(PAIRS):
+            amp_t_psum = flipped.tile([P, P], F32, name="amp_t_psum")
+            nc.tensor.transpose(out=amp_t_psum[:], in_=amp_pairs[j][:].rearrange("p b m -> p (b m)"), identity=identity[:])
+            amp_t = held.tile([P, P], F32, name=f"amp_t{j}")
+            nc.scalar.copy(out=amp_t[:], in_=amp_t_psum[:])
+            for h in range(2):
+                b = 2 * j + h
+                coef_psum = sums.tile([P, S], F32, name="coef_psum")
+                nc.tensor.matmul(out=coef_psum[:], lhsT=amp_t[:], rhs=wave_diag[:, h * S : (h + 1) * S],
+                                 start=True, stop=True)
+                coef = held.tile([P, S], F32, name=f"coef{b}")
+                nc.scalar.copy(out=coef[:], in_=coef_psum[:])
+                for k in range(PIECES):
+                    product = products.tile([P, S], F32, name="product")
+                    picked = tables[b][:].indirect(offsets[:, k * (S // 16) : (k + 1) * (S // 16)])
+                    nc.vector.tensor_tensor(out=product[:], in0=picked, in1=coef[:], op=ALU.mult)
+                    nc.sync.dma_start(out[b * P : (b + 1) * P, k * S : (k + 1) * S], product[:])

@@ -29,7 +29,7 @@ def tile_waveencoder_kernel(tc, x, amp, freq, offs, out):
         tc.tile_pool(name="held", bufs=1) as held,
         tc.tile_pool(name="products", bufs=8) as products,
         tc.psum_pool(name="flipped", bufs=2) as flipped,
-        tc.psum_pool(name="sums", bufs=4) as sums,
+        tc.psum_pool(name="sums", bufs=3) as sums,
     ):
         freq_col = held.tile([P, 1], F32, name="freq_col")
         with nc.allow_non_contiguous_dma(reason="64 frequencies, one to a partition"):
@@ -38,23 +38,23 @@ def tile_waveencoder_kernel(tc, x, amp, freq, offs, out):
         offsets = held.tile([P, N // 16], U16, name="offsets")
         nc.sync.dma_start(offsets[:], offs)
         amp_pairs = []
+        tables = []
         for j in range(PAIRS):
             amp_pair = held.tile([P, 2, F], F32, name=f"amp_pair{j}")
-            nc.scalar.dma_start(amp_pair[:], amp[2 * j * P : (2 * j + 2) * P, :].rearrange("(b p) m -> p b m", p=P))
+            nc.sync.dma_start(amp_pair[:], amp[2 * j * P : (2 * j + 2) * P, :].rearrange("(b p) m -> p b m", p=P))
             amp_pairs.append(amp_pair)
-        tables = []
-        for b in range(BLOCKS):
-            table = held.tile([P, S], F32, name=f"table{b}")
-            nc.sync.dma_start(table[:], x[b * P : (b + 1) * P, :])
-            tables.append(table)
+            for b in (2 * j, 2 * j + 1):
+                table = held.tile([P, S], F32, name=f"table{b}")
+                nc.sync.dma_start(table[:], x[b * P : (b + 1) * P, :])
+                tables.append(table)
 
-        identity = held.tile([P, P], F32, name="identity")
-        make_identity(nc, identity[:])
         position = held.tile([P, S + QUARTER], F32, name="position")
         nc.gpsimd.iota(position[:, 0 : S // 2], pattern=[[1, S // 2]], base=0, channel_multiplier=0,
                        allow_small_or_imprecise_dtypes=True)
         nc.gpsimd.iota(position[:, S // 2 :], pattern=[[1, S // 2 + QUARTER]], base=-(S // 2), channel_multiplier=0,
                        allow_small_or_imprecise_dtypes=True)
+        identity = held.tile([P, P], F32, name="identity")
+        make_identity(nc, identity[:])
         sine = held.tile([P, S + QUARTER], F32, name="sine")
         nc.scalar.activation(out=sine[:], in_=position[:], func=ACT.Sin, scale=TWO_PI / S)
         sin_a = sine[:, 0:S]
@@ -63,8 +63,10 @@ def tile_waveencoder_kernel(tc, x, amp, freq, offs, out):
         nc.vector.memset(phase[:, 0:1], 0.25)
         nc.vector.memset(phase[:, 1:2], 0.0)
         wave_diag = held.tile([P, 2 * S], F32, name="wave_diag")
-        nc.gpsimd.memset(wave_diag[0:F, S : 2 * S], 0.0)
-        nc.gpsimd.memset(wave_diag[F:P, 0:S], 0.0)
+        nc.vector.memset(wave_diag[0:F, S : 2 * S], 0.0)
+        nc.vector.memset(wave_diag[F:P, 0:S], 0.0)
+        cos_sin_first = held.tile([P, 2], F32, name="cos_sin_first")
+        nc.vector.memset(cos_sin_first[:], 0.0)
 
         whole = held.tile([P, 1], I32, name="whole")
         nc.vector.tensor_copy(whole[:], freq_col[:])
@@ -75,8 +77,20 @@ def tile_waveencoder_kernel(tc, x, amp, freq, offs, out):
         fold(nc, folded_once[:], minus_turns[:])
         folded = held.tile([P, 2], F32, name="folded")
         fold(nc, folded[:], folded_once[:])
+        nc.scalar.activation(out=cos_sin_first[0:F, :], in_=folded[0:F, :], func=ACT.Sin, scale=-TWO_PI)
         cos_sin_th = held.tile([P, 2], F32, name="cos_sin_th")
         nc.scalar.activation(out=cos_sin_th[:], in_=folded[:], func=ACT.Sin, scale=-TWO_PI)
+
+        def flip_amp(j):
+            amp_t_psum = flipped.tile([P, P], F32, name="amp_t_psum")
+            nc.tensor.transpose(out=amp_t_psum[:], in_=amp_pairs[j][:].rearrange("p b m -> p (b m)"), identity=identity[:])
+            amp_t = held.tile([P, P], F32, name=f"amp_t{j}")
+            nc.scalar.copy(out=amp_t[:], in_=amp_t_psum[:])
+            return amp_t
+
+        amp_t = flip_amp(0)
+        p_q = flipped.tile([P, 2], F32, name="p_q")
+        nc.tensor.matmul(out=p_q[:], lhsT=amp_t[:], rhs=cos_sin_first[:], start=True, stop=True)
 
         cos_part = held.tile([P, S], F32, name="cos_part")
         nc.vector.tensor_scalar(out=cos_part[:], in0=cos_a, scalar1=cos_sin_th[:, 0:1], scalar2=None, op0=ALU.mult)
@@ -86,20 +100,26 @@ def tile_waveencoder_kernel(tc, x, amp, freq, offs, out):
                                            scalar=cos_sin_th[rows, 1:2], in1=cos_part[rows, :],
                                            op0=ALU.mult, op1=ALU.add)
 
-        for j in range(PAIRS):
-            amp_t_psum = flipped.tile([P, P], F32, name="amp_t_psum")
-            nc.tensor.transpose(out=amp_t_psum[:], in_=amp_pairs[j][:].rearrange("p b m -> p (b m)"), identity=identity[:])
-            amp_t = held.tile([P, P], F32, name=f"amp_t{j}")
-            nc.scalar.copy(out=amp_t[:], in_=amp_t_psum[:])
-            for h in range(2):
-                b = 2 * j + h
-                coef_psum = sums.tile([P, S], F32, name="coef_psum")
-                nc.tensor.matmul(out=coef_psum[:], lhsT=amp_t[:], rhs=wave_diag[:, h * S : (h + 1) * S],
-                                 start=True, stop=True)
-                coef = held.tile([P, S], F32, name=f"coef{b}")
-                nc.scalar.copy(out=coef[:], in_=coef_psum[:])
-                for k in range(PIECES):
-                    product = products.tile([P, S], F32, name="product")
-                    picked = tables[b][:].indirect(offsets[:, k * (S // 16) : (k + 1) * (S // 16)])
-                    nc.vector.tensor_tensor(out=product[:], in0=picked, in1=coef[:], op=ALU.mult)
-                    nc.sync.dma_start(out[b * P : (b + 1) * P, k * S : (k + 1) * S], product[:])
+        coefs = []
+        p_cos = held.tile([P, S], F32, name="p_cos")
+        nc.vector.tensor_scalar(out=p_cos[:], in0=cos_a, scalar1=p_q[:, 0:1], scalar2=None, op0=ALU.mult)
+        coef = held.tile([P, S], F32, name="coef0")
+        nc.vector.scalar_tensor_tensor(out=coef[:], in0=sin_a, scalar=p_q[:, 1:2], in1=p_cos[:], op0=ALU.mult, op1=ALU.add)
+        coefs.append(coef)
+
+        for b in range(1, BLOCKS):
+            j, h = divmod(b, 2)
+            if h == 0:
+                amp_t = flip_amp(j)
+            coef_psum = sums.tile([P, S], F32, name="coef_psum")
+            nc.tensor.matmul(out=coef_psum[:], lhsT=amp_t[:], rhs=wave_diag[:, h * S : (h + 1) * S], start=True, stop=True)
+            coef = held.tile([P, S], F32, name=f"coef{b}")
+            nc.scalar.copy(out=coef[:], in_=coef_psum[:])
+            coefs.append(coef)
+
+        for b in range(BLOCKS):
+            for k in range(PIECES):
+                product = products.tile([P, S], F32, name="product")
+                picked = tables[b][:].indirect(offsets[:, k * (S // 16) : (k + 1) * (S // 16)])
+                nc.vector.tensor_tensor(out=product[:], in0=picked, in1=coefs[b][:], op=ALU.mult)
+                nc.sync.dma_start(out[b * P : (b + 1) * P, k * S : (k + 1) * S], product[:])

@@ -27,7 +27,7 @@ def tile_waveencoder_kernel(tc, x, amp, freq, offs, out):
     nc = tc.nc
     with (
         tc.tile_pool(name="held", bufs=1) as held,
-        tc.tile_pool(name="products", bufs=8) as products,
+        tc.tile_pool(name="products", bufs=BLOCKS * PIECES) as products,
         tc.psum_pool(name="flipped", bufs=2) as flipped,
         tc.psum_pool(name="sums", bufs=3) as sums,
     ):

@@ -27,7 +27,7 @@ def tile_waveencoder_kernel(tc, x, amp, freq, offs, out):
     nc = tc.nc
     with (
         tc.tile_pool(name="held", bufs=1) as held,
-        tc.tile_pool(name="products", bufs=BLOCKS * PIECES) as products,
+        tc.tile_pool(name="products", bufs=8) as products,
         tc.psum_pool(name="flipped", bufs=2) as flipped,
         tc.psum_pool(name="sums", bufs=3) as sums,
     ):
@@ -38,15 +38,15 @@ def tile_waveencoder_kernel(tc, x, amp, freq, offs, out):
         offsets = held.tile([P, N // 16], U16, name="offsets")
         nc.sync.dma_start(offsets[:], offs)
         amp_pairs = []
-        tables = []
         for j in range(PAIRS):
             amp_pair = held.tile([P, 2, F], F32, name=f"amp_pair{j}")
-            nc.sync.dma_start(amp_pair[:], amp[2 * j * P : (2 * j + 2) * P, :].rearrange("(b p) m -> p b m", p=P))
+            nc.scalar.dma_start(amp_pair[:], amp[2 * j * P : (2 * j + 2) * P, :].rearrange("(b p) m -> p b m", p=P))
             amp_pairs.append(amp_pair)
-            for b in (2 * j, 2 * j + 1):
-                table = held.tile([P, S], F32, name=f"table{b}")
-                nc.sync.dma_start(table[:], x[b * P : (b + 1) * P, :])
-                tables.append(table)
+        tables = []
+        for b in range(BLOCKS):
+            table = held.tile([P, S], F32, name=f"table{b}")
+            nc.sync.dma_start(table[:], x[b * P : (b + 1) * P, :])
+            tables.append(table)
 
         position = held.tile([P, S + QUARTER], F32, name="position")
         nc.gpsimd.iota(position[:, 0 : S // 2], pattern=[[1, S // 2]], base=0, channel_multiplier=0,
@@ -118,8 +118,10 @@ def tile_waveencoder_kernel(tc, x, amp, freq, offs, out):
             coefs.append(coef)
 
         for b in range(BLOCKS):
-            for k in range(PIECES):
-                product = products.tile([P, S], F32, name="product")
-                picked = tables[b][:].indirect(offsets[:, k * (S // 16) : (k + 1) * (S // 16)])
-                nc.vector.tensor_tensor(out=product[:], in0=picked, in1=coefs[b][:], op=ALU.mult)
-                nc.sync.dma_start(out[b * P : (b + 1) * P, k * S : (k + 1) * S], product[:])
+            for half, queue in enumerate((nc.sync, nc.scalar)):
+                product = products.tile([P, 2 * S], F32, name="product")
+                for i in range(2):
+                    k = 2 * half + i
+                    picked = tables[b][:].indirect(offsets[:, k * (S // 16) : (k + 1) * (S // 16)])
+                    nc.vector.tensor_tensor(out=product[:, i * S : (i + 1) * S], in0=picked, in1=coefs[b][:], op=ALU.mult)
+                queue.dma_start(out[b * P : (b + 1) * P, 2 * half * S : 2 * (half + 1) * S], product[:])

@@ -4,6 +4,7 @@ from concourse.masks import make_identity
 F32 = mybir.dt.float32
 I32 = mybir.dt.int32
 U16 = mybir.dt.uint16
+U32 = mybir.dt.uint32
 ALU = mybir.AluOpType
 ACT = mybir.ActivationFunctionType
 
@@ -15,12 +16,9 @@ PIECES = N // S
 QUARTER = S // 4
 
 TWO_PI = 6.283185
+TURN = 1 << 22
 
 FLOPS = 2 * C * F * S + C * N
-
-
-def fold(nc, out, turns):
-    nc.vector.scalar_tensor_tensor(out=out, in0=turns, scalar=0.5, in1=turns, op0=ALU.is_gt, op1=ALU.subtract)
 
 
 def tile_waveencoder_kernel(tc, x, amp, freq, offs, out):
@@ -60,26 +58,28 @@ def tile_waveencoder_kernel(tc, x, amp, freq, offs, out):
         sin_a = sine[:, 0:S]
         cos_a = sine[:, QUARTER : QUARTER + S]
         phase = held.tile([P, 2], F32, name="phase")
-        nc.vector.memset(phase[:, 0:1], 0.25)
-        nc.vector.memset(phase[:, 1:2], 0.0)
-        wave_diag = held.tile([P, 2 * S], F32, name="wave_diag")
-        nc.vector.memset(wave_diag[0:F, S : 2 * S], 0.0)
-        nc.vector.memset(wave_diag[F:P, 0:S], 0.0)
+        nc.vector.memset(phase[:, 0:1], float(3 * TURN // 4))
+        nc.vector.memset(phase[:, 1:2], float(TURN // 2))
+        minus_half_turn = held.tile([P, 1], F32, name="minus_half_turn")
+        nc.vector.memset(minus_half_turn[:], -TWO_PI / 2)
+        cos_diag = held.tile([P, 2 * S], F32, name="cos_diag")
+        sin_diag = held.tile([P, 2 * S], F32, name="sin_diag")
+        for diag in (cos_diag, sin_diag):
+            nc.vector.memset(diag[0:F, S : 2 * S], 0.0)
+            nc.vector.memset(diag[F:P, 0:S], 0.0)
         cos_sin_first = held.tile([P, 2], F32, name="cos_sin_first")
         nc.vector.memset(cos_sin_first[:], 0.0)
 
-        whole = held.tile([P, 1], I32, name="whole")
-        nc.vector.tensor_copy(whole[:], freq_col[:])
-        minus_turns = held.tile([P, 2], F32, name="minus_turns")
-        nc.vector.scalar_tensor_tensor(out=minus_turns[:], in0=whole[:, 0:1].to_broadcast([P, 2]), scalar=freq_col[:, 0:1],
-                                       in1=phase[:], op0=ALU.subtract, op1=ALU.subtract)
-        folded_once = held.tile([P, 2], F32, name="folded_once")
-        fold(nc, folded_once[:], minus_turns[:])
-        folded = held.tile([P, 2], F32, name="folded")
-        fold(nc, folded[:], folded_once[:])
-        nc.scalar.activation(out=cos_sin_first[0:F, :], in_=folded[0:F, :], func=ACT.Sin, scale=-TWO_PI)
+        turns = held.tile([P, 2], I32, name="turns")
+        nc.vector.scalar_tensor_tensor(out=turns[:], in0=freq_col[:, 0:1].to_broadcast([P, 2]), scalar=float(TURN),
+                                       in1=phase[:], op0=ALU.mult, op1=ALU.add)
+        fraction = held.tile([P, 2], I32, name="fraction")
+        nc.vector.tensor_scalar(out=fraction[:], in0=turns[:], scalar1=TURN - 1, scalar2=None, op0=ALU.bitwise_and)
+        angle = fraction[:].bitcast(U32)
+        nc.scalar.activation(out=cos_sin_first[0:F, :], in_=angle[0:F, :], func=ACT.Sin, scale=TWO_PI / TURN,
+                             bias=minus_half_turn[0:F, :])
         cos_sin_th = held.tile([P, 2], F32, name="cos_sin_th")
-        nc.scalar.activation(out=cos_sin_th[:], in_=folded[:], func=ACT.Sin, scale=-TWO_PI)
+        nc.scalar.activation(out=cos_sin_th[:], in_=angle, func=ACT.Sin, scale=TWO_PI / TURN, bias=minus_half_turn[:])
 
         def flip_amp(j):
             amp_t_psum = flipped.tile([P, P], F32, name="amp_t_psum")
@@ -92,13 +92,11 @@ def tile_waveencoder_kernel(tc, x, amp, freq, offs, out):
         p_q = flipped.tile([P, 2], F32, name="p_q")
         nc.tensor.matmul(out=p_q[:], lhsT=amp_t[:], rhs=cos_sin_first[:], start=True, stop=True)
 
-        cos_part = held.tile([P, S], F32, name="cos_part")
-        nc.vector.tensor_scalar(out=cos_part[:], in0=cos_a, scalar1=cos_sin_th[:, 0:1], scalar2=None, op0=ALU.mult)
-        for h in range(2):
+        for h in (1, 0):
             rows = slice(h * F, (h + 1) * F)
-            nc.vector.scalar_tensor_tensor(out=wave_diag[rows, h * S : (h + 1) * S], in0=sin_a[rows, :],
-                                           scalar=cos_sin_th[rows, 1:2], in1=cos_part[rows, :],
-                                           op0=ALU.mult, op1=ALU.add)
+            cols = slice(h * S, (h + 1) * S)
+            nc.scalar.activation(out=cos_diag[rows, cols], in_=cos_a[rows, :], func=ACT.Copy, scale=cos_sin_th[rows, 0:1])
+            nc.scalar.activation(out=sin_diag[rows, cols], in_=sin_a[rows, :], func=ACT.Copy, scale=cos_sin_th[rows, 1:2])
 
         coefs = []
         p_cos = held.tile([P, S], F32, name="p_cos")
@@ -112,7 +110,8 @@ def tile_waveencoder_kernel(tc, x, amp, freq, offs, out):
             if h == 0:
                 amp_t = flip_amp(j)
             coef_psum = sums.tile([P, S], F32, name="coef_psum")
-            nc.tensor.matmul(out=coef_psum[:], lhsT=amp_t[:], rhs=wave_diag[:, h * S : (h + 1) * S], start=True, stop=True)
+            nc.tensor.matmul(out=coef_psum[:], lhsT=amp_t[:], rhs=cos_diag[:, h * S : (h + 1) * S], start=True, stop=False)
+            nc.tensor.matmul(out=coef_psum[:], lhsT=amp_t[:], rhs=sin_diag[:, h * S : (h + 1) * S], start=False, stop=True)
             coef = held.tile([P, S], F32, name=f"coef{b}")
             nc.scalar.copy(out=coef[:], in_=coef_psum[:])
             coefs.append(coef)

@@ -4,7 +4,6 @@ from concourse.masks import make_identity
 F32 = mybir.dt.float32
 I32 = mybir.dt.int32
 U16 = mybir.dt.uint16
-U32 = mybir.dt.uint32
 ALU = mybir.AluOpType
 ACT = mybir.ActivationFunctionType
 
@@ -16,16 +15,19 @@ PIECES = N // S
 QUARTER = S // 4
 
 TWO_PI = 6.283185
-TURN = 1 << 22
 
 FLOPS = 2 * C * F * S + C * N
+
+
+def fold(nc, out, turns):
+    nc.vector.scalar_tensor_tensor(out=out, in0=turns, scalar=0.5, in1=turns, op0=ALU.is_gt, op1=ALU.subtract)
 
 
 def tile_waveencoder_kernel(tc, x, amp, freq, offs, out):
     nc = tc.nc
     with (
         tc.tile_pool(name="held", bufs=1) as held,
-        tc.tile_pool(name="products", bufs=8) as products,
+        tc.tile_pool(name="products", bufs=4) as products,
         tc.psum_pool(name="flipped", bufs=2) as flipped,
         tc.psum_pool(name="sums", bufs=3) as sums,
     ):
@@ -58,28 +60,26 @@ def tile_waveencoder_kernel(tc, x, amp, freq, offs, out):
         sin_a = sine[:, 0:S]
         cos_a = sine[:, QUARTER : QUARTER + S]
         phase = held.tile([P, 2], F32, name="phase")
-        nc.vector.memset(phase[:, 0:1], float(3 * TURN // 4))
-        nc.vector.memset(phase[:, 1:2], float(TURN // 2))
-        minus_half_turn = held.tile([P, 1], F32, name="minus_half_turn")
-        nc.vector.memset(minus_half_turn[:], -TWO_PI / 2)
-        cos_diag = held.tile([P, 2 * S], F32, name="cos_diag")
-        sin_diag = held.tile([P, 2 * S], F32, name="sin_diag")
-        for diag in (cos_diag, sin_diag):
-            nc.vector.memset(diag[0:F, S : 2 * S], 0.0)
-            nc.vector.memset(diag[F:P, 0:S], 0.0)
+        nc.vector.memset(phase[:, 0:1], 0.25)
+        nc.vector.memset(phase[:, 1:2], 0.0)
+        wave_diag = held.tile([P, 2 * S], F32, name="wave_diag")
+        nc.vector.memset(wave_diag[0:F, S : 2 * S], 0.0)
+        nc.vector.memset(wave_diag[F:P, 0:S], 0.0)
         cos_sin_first = held.tile([P, 2], F32, name="cos_sin_first")
         nc.vector.memset(cos_sin_first[:], 0.0)
 
-        turns = held.tile([P, 2], I32, name="turns")
-        nc.vector.scalar_tensor_tensor(out=turns[:], in0=freq_col[:, 0:1].to_broadcast([P, 2]), scalar=float(TURN),
-                                       in1=phase[:], op0=ALU.mult, op1=ALU.add)
-        fraction = held.tile([P, 2], I32, name="fraction")
-        nc.vector.tensor_scalar(out=fraction[:], in0=turns[:], scalar1=TURN - 1, scalar2=None, op0=ALU.bitwise_and)
-        angle = fraction[:].bitcast(U32)
-        nc.scalar.activation(out=cos_sin_first[0:F, :], in_=angle[0:F, :], func=ACT.Sin, scale=TWO_PI / TURN,
-                             bias=minus_half_turn[0:F, :])
+        whole = held.tile([P, 1], I32, name="whole")
+        nc.vector.tensor_copy(whole[:], freq_col[:])
+        minus_turns = held.tile([P, 2], F32, name="minus_turns")
+        nc.vector.scalar_tensor_tensor(out=minus_turns[:], in0=whole[:, 0:1].to_broadcast([P, 2]), scalar=freq_col[:, 0:1],
+                                       in1=phase[:], op0=ALU.subtract, op1=ALU.subtract)
+        folded_once = held.tile([P, 2], F32, name="folded_once")
+        fold(nc, folded_once[:], minus_turns[:])
+        folded = held.tile([P, 2], F32, name="folded")
+        fold(nc, folded[:], folded_once[:])
+        nc.scalar.activation(out=cos_sin_first[0:F, :], in_=folded[0:F, :], func=ACT.Sin, scale=-TWO_PI)
         cos_sin_th = held.tile([P, 2], F32, name="cos_sin_th")
-        nc.scalar.activation(out=cos_sin_th[:], in_=angle, func=ACT.Sin, scale=TWO_PI / TURN, bias=minus_half_turn[:])
+        nc.scalar.activation(out=cos_sin_th[:], in_=folded[:], func=ACT.Sin, scale=-TWO_PI)
 
         def flip_amp(j):
             amp_t_psum = flipped.tile([P, P], F32, name="amp_t_psum")
@@ -92,11 +92,13 @@ def tile_waveencoder_kernel(tc, x, amp, freq, offs, out):
         p_q = flipped.tile([P, 2], F32, name="p_q")
         nc.tensor.matmul(out=p_q[:], lhsT=amp_t[:], rhs=cos_sin_first[:], start=True, stop=True)
 
-        for h in (1, 0):
+        cos_part = held.tile([P, S], F32, name="cos_part")
+        nc.vector.tensor_scalar(out=cos_part[:], in0=cos_a, scalar1=cos_sin_th[:, 0:1], scalar2=None, op0=ALU.mult)
+        for h in range(2):
             rows = slice(h * F, (h + 1) * F)
-            cols = slice(h * S, (h + 1) * S)
-            nc.scalar.activation(out=cos_diag[rows, cols], in_=cos_a[rows, :], func=ACT.Copy, scale=cos_sin_th[rows, 0:1])
-            nc.scalar.activation(out=sin_diag[rows, cols], in_=sin_a[rows, :], func=ACT.Copy, scale=cos_sin_th[rows, 1:2])
+            nc.vector.scalar_tensor_tensor(out=wave_diag[rows, h * S : (h + 1) * S], in0=sin_a[rows, :],
+                                           scalar=cos_sin_th[rows, 1:2], in1=cos_part[rows, :],
+                                           op0=ALU.mult, op1=ALU.add)
 
         coefs = []
         p_cos = held.tile([P, S], F32, name="p_cos")
@@ -110,17 +112,20 @@ def tile_waveencoder_kernel(tc, x, amp, freq, offs, out):
             if h == 0:
                 amp_t = flip_amp(j)
             coef_psum = sums.tile([P, S], F32, name="coef_psum")
-            nc.tensor.matmul(out=coef_psum[:], lhsT=amp_t[:], rhs=cos_diag[:, h * S : (h + 1) * S], start=True, stop=False)
-            nc.tensor.matmul(out=coef_psum[:], lhsT=amp_t[:], rhs=sin_diag[:, h * S : (h + 1) * S], start=False, stop=True)
+            nc.tensor.matmul(out=coef_psum[:], lhsT=amp_t[:], rhs=wave_diag[:, h * S : (h + 1) * S], start=True, stop=True)
             coef = held.tile([P, S], F32, name=f"coef{b}")
             nc.scalar.copy(out=coef[:], in_=coef_psum[:])
             coefs.append(coef)
 
+        queues = (nc.sync, nc.scalar)
+        stores = 0
         for b in range(BLOCKS):
-            for half, queue in enumerate((nc.sync, nc.scalar)):
-                product = products.tile([P, 2 * S], F32, name="product")
-                for i in range(2):
-                    k = 2 * half + i
-                    picked = tables[b][:].indirect(offsets[:, k * (S // 16) : (k + 1) * (S // 16)])
-                    nc.vector.tensor_tensor(out=product[:, i * S : (i + 1) * S], in0=picked, in1=coefs[b][:], op=ALU.mult)
-                queue.dma_start(out[b * P : (b + 1) * P, 2 * half * S : 2 * (half + 1) * S], product[:])
+            product = products.tile([P, N], F32, name="product")
+            pieces_a_store = PIECES if b < BLOCKS - 1 else PIECES // 2
+            for k in range(PIECES):
+                picked = tables[b][:].indirect(offsets[:, k * (S // 16) : (k + 1) * (S // 16)])
+                nc.vector.tensor_tensor(out=product[:, k * S : (k + 1) * S], in0=picked, in1=coefs[b][:], op=ALU.mult)
+                if (k + 1) % pieces_a_store == 0:
+                    done = slice((k + 1 - pieces_a_store) * S, (k + 1) * S)
+                    queues[stores % 2].dma_start(out[b * P : (b + 1) * P, done], product[:, done])
+                    stores += 1

@@ -27,14 +27,14 @@ def tile_waveencoder_kernel(tc, x, amp, freq, offs, out):
     nc = tc.nc
     with (
         tc.tile_pool(name="held", bufs=1) as held,
-        tc.tile_pool(name="products", bufs=4) as products,
+        tc.tile_pool(name="products", bufs=8) as products,
         tc.psum_pool(name="flipped", bufs=2) as flipped,
         tc.psum_pool(name="sums", bufs=3) as sums,
     ):
         freq_col = held.tile([P, 1], F32, name="freq_col")
         with nc.allow_non_contiguous_dma(reason="64 frequencies, one to a partition"):
             nc.sync.dma_start(freq_col[0:F, :], freq.rearrange("o m -> m o"))
-            nc.scalar.dma_start(freq_col[F:P, :], freq.rearrange("o m -> m o"))
+            nc.sync.dma_start(freq_col[F:P, :], freq.rearrange("o m -> m o"))
         offsets = held.tile([P, N // 16], U16, name="offsets")
         nc.sync.dma_start(offsets[:], offs)
         amp_pairs = []
@@ -117,15 +117,11 @@ def tile_waveencoder_kernel(tc, x, amp, freq, offs, out):
             nc.scalar.copy(out=coef[:], in_=coef_psum[:])
             coefs.append(coef)
 
-        queues = (nc.sync, nc.scalar)
-        stores = 0
         for b in range(BLOCKS):
-            product = products.tile([P, N], F32, name="product")
-            pieces_a_store = PIECES if b < BLOCKS - 1 else PIECES // 2
-            for k in range(PIECES):
-                picked = tables[b][:].indirect(offsets[:, k * (S // 16) : (k + 1) * (S // 16)])
-                nc.vector.tensor_tensor(out=product[:, k * S : (k + 1) * S], in0=picked, in1=coefs[b][:], op=ALU.mult)
-                if (k + 1) % pieces_a_store == 0:
-                    done = slice((k + 1 - pieces_a_store) * S, (k + 1) * S)
-                    queues[stores % 2].dma_start(out[b * P : (b + 1) * P, done], product[:, done])
-                    stores += 1
+            for half, queue in enumerate((nc.sync, nc.scalar)):
+                product = products.tile([P, 2 * S], F32, name="product")
+                for i in range(2):
+                    k = 2 * half + i
+                    picked = tables[b][:].indirect(offsets[:, k * (S // 16) : (k + 1) * (S // 16)])
+                    nc.vector.tensor_tensor(out=product[:, i * S : (i + 1) * S], in0=picked, in1=coefs[b][:], op=ALU.mult)
+                queue.dma_start(out[b * P : (b + 1) * P, 2 * half * S : 2 * (half + 1) * S], product[:])

@@ -4,23 +4,20 @@ from concourse.masks import make_identity
 F32 = mybir.dt.float32
 I32 = mybir.dt.int32
 U16 = mybir.dt.uint16
+U32 = mybir.dt.uint32
 ALU = mybir.AluOpType
 ACT = mybir.ActivationFunctionType
 
 P = 128
 C, S, F, N = 1024, 256, 64, 1024
 BLOCKS = C // P
-PAIRS = BLOCKS // 2
 PIECES = N // S
 QUARTER = S // 4
 
 TWO_PI = 6.283185
+TURN = 1 << 22
 
 FLOPS = 2 * C * F * S + C * N
-
-
-def fold(nc, out, turns):
-    nc.vector.scalar_tensor_tensor(out=out, in0=turns, scalar=0.5, in1=turns, op0=ALU.is_gt, op1=ALU.subtract)
 
 
 def tile_waveencoder_kernel(tc, x, amp, freq, offs, out):
@@ -31,21 +28,21 @@ def tile_waveencoder_kernel(tc, x, amp, freq, offs, out):
         tc.psum_pool(name="flipped", bufs=2) as flipped,
         tc.psum_pool(name="sums", bufs=3) as sums,
     ):
-        freq_col = held.tile([P, 1], F32, name="freq_col")
+        freq_col = held.tile([F, 1], F32, name="freq_col")
         with nc.allow_non_contiguous_dma(reason="64 frequencies, one to a partition"):
-            nc.sync.dma_start(freq_col[0:F, :], freq.rearrange("o m -> m o"))
-            nc.sync.dma_start(freq_col[F:P, :], freq.rearrange("o m -> m o"))
+            nc.sync.dma_start(freq_col[:], freq.rearrange("o m -> m o"))
         offsets = held.tile([P, N // 16], U16, name="offsets")
         nc.sync.dma_start(offsets[:], offs)
-        amp_pairs = []
-        for j in range(PAIRS):
-            amp_pair = held.tile([P, 2, F], F32, name=f"amp_pair{j}")
-            nc.scalar.dma_start(amp_pair[:], amp[2 * j * P : (2 * j + 2) * P, :].rearrange("(b p) m -> p b m", p=P))
-            amp_pairs.append(amp_pair)
+        amp_wide = held.tile([P, BLOCKS, 2 * F], F32, name="amp_wide")
+        amp_blocks = amp.rearrange("(b p) m -> p b m", p=P)
+        nc.vector.memset(amp_wide[:, :, F : 2 * F], 0.0)
+        nc.scalar.dma_start(amp_wide[:, 0:1, 0:F], amp_blocks[:, 0:1, :])
+        nc.sync.dma_start(amp_wide[:, 1:BLOCKS, 0:F], amp_blocks[:, 1:BLOCKS, :])
         tables = []
         for b in range(BLOCKS):
             table = held.tile([P, S], F32, name=f"table{b}")
-            nc.sync.dma_start(table[:], x[b * P : (b + 1) * P, :])
+            queue = nc.scalar if b == 0 else nc.sync
+            queue.dma_start(table[:], x[b * P : (b + 1) * P, :])
             tables.append(table)
 
         position = held.tile([P, S + QUARTER], F32, name="position")
@@ -54,51 +51,44 @@ def tile_waveencoder_kernel(tc, x, amp, freq, offs, out):
         nc.gpsimd.iota(position[:, S // 2 :], pattern=[[1, S // 2 + QUARTER]], base=-(S // 2), channel_multiplier=0,
                        allow_small_or_imprecise_dtypes=True)
         identity = held.tile([P, P], F32, name="identity")
-        make_identity(nc, identity[:])
+        nc.vector.memset(identity[:], 0.0)
+        make_identity(nc, identity[:], nomemset=True)
         sine = held.tile([P, S + QUARTER], F32, name="sine")
         nc.scalar.activation(out=sine[:], in_=position[:], func=ACT.Sin, scale=TWO_PI / S)
         sin_a = sine[:, 0:S]
         cos_a = sine[:, QUARTER : QUARTER + S]
-        phase = held.tile([P, 2], F32, name="phase")
-        nc.vector.memset(phase[:, 0:1], 0.25)
-        nc.vector.memset(phase[:, 1:2], 0.0)
-        wave_diag = held.tile([P, 2 * S], F32, name="wave_diag")
-        nc.vector.memset(wave_diag[0:F, S : 2 * S], 0.0)
-        nc.vector.memset(wave_diag[F:P, 0:S], 0.0)
-        cos_sin_first = held.tile([P, 2], F32, name="cos_sin_first")
-        nc.vector.memset(cos_sin_first[:], 0.0)
-
-        whole = held.tile([P, 1], I32, name="whole")
-        nc.vector.tensor_copy(whole[:], freq_col[:])
-        minus_turns = held.tile([P, 2], F32, name="minus_turns")
-        nc.vector.scalar_tensor_tensor(out=minus_turns[:], in0=whole[:, 0:1].to_broadcast([P, 2]), scalar=freq_col[:, 0:1],
-                                       in1=phase[:], op0=ALU.subtract, op1=ALU.subtract)
-        folded_once = held.tile([P, 2], F32, name="folded_once")
-        fold(nc, folded_once[:], minus_turns[:])
-        folded = held.tile([P, 2], F32, name="folded")
-        fold(nc, folded[:], folded_once[:])
-        nc.scalar.activation(out=cos_sin_first[0:F, :], in_=folded[0:F, :], func=ACT.Sin, scale=-TWO_PI)
+        phase = held.tile([F, 2], F32, name="phase")
+        nc.vector.memset(phase[:, 0:1], float(3 * TURN // 4))
+        nc.vector.memset(phase[:, 1:2], float(TURN // 2))
+        minus_half_turn = held.tile([F, 1], F32, name="minus_half_turn")
+        nc.vector.memset(minus_half_turn[:], -TWO_PI / 2)
         cos_sin_th = held.tile([P, 2], F32, name="cos_sin_th")
-        nc.scalar.activation(out=cos_sin_th[:], in_=folded[:], func=ACT.Sin, scale=-TWO_PI)
+        nc.vector.memset(cos_sin_th[F:P, :], 0.0)
+        wave = held.tile([P, S], F32, name="wave")
+        nc.vector.memset(wave[F:P, :], 0.0)
 
-        def flip_amp(j):
+        turns = held.tile([F, 2], I32, name="turns")
+        nc.vector.scalar_tensor_tensor(out=turns[:], in0=freq_col[:, 0:1].to_broadcast([F, 2]), scalar=float(TURN),
+                                       in1=phase[:], op0=ALU.mult, op1=ALU.add)
+        fraction = held.tile([F, 2], I32, name="fraction")
+        nc.vector.tensor_scalar(out=fraction[:], in0=turns[:], scalar1=TURN - 1, scalar2=None, op0=ALU.bitwise_and)
+        nc.scalar.activation(out=cos_sin_th[0:F, :], in_=fraction[:].bitcast(U32), func=ACT.Sin, scale=TWO_PI / TURN,
+                             bias=minus_half_turn[:])
+
+        def flip_amp(b):
             amp_t_psum = flipped.tile([P, P], F32, name="amp_t_psum")
-            nc.tensor.transpose(out=amp_t_psum[:], in_=amp_pairs[j][:].rearrange("p b m -> p (b m)"), identity=identity[:])
-            amp_t = held.tile([P, P], F32, name=f"amp_t{j}")
+            nc.tensor.transpose(out=amp_t_psum[:], in_=amp_wide[:, b, :], identity=identity[:])
+            amp_t = held.tile([P, P], F32, name=f"amp_t{b}")
             nc.scalar.copy(out=amp_t[:], in_=amp_t_psum[:])
             return amp_t
 
-        amp_t = flip_amp(0)
         p_q = flipped.tile([P, 2], F32, name="p_q")
-        nc.tensor.matmul(out=p_q[:], lhsT=amp_t[:], rhs=cos_sin_first[:], start=True, stop=True)
+        nc.tensor.matmul(out=p_q[:], lhsT=flip_amp(0)[:], rhs=cos_sin_th[:], start=True, stop=True)
 
-        cos_part = held.tile([P, S], F32, name="cos_part")
-        nc.vector.tensor_scalar(out=cos_part[:], in0=cos_a, scalar1=cos_sin_th[:, 0:1], scalar2=None, op0=ALU.mult)
-        for h in range(2):
-            rows = slice(h * F, (h + 1) * F)
-            nc.vector.scalar_tensor_tensor(out=wave_diag[rows, h * S : (h + 1) * S], in0=sin_a[rows, :],
-                                           scalar=cos_sin_th[rows, 1:2], in1=cos_part[rows, :],
-                                           op0=ALU.mult, op1=ALU.add)
+        cos_part = held.tile([F, S], F32, name="cos_part")
+        nc.vector.tensor_scalar(out=cos_part[:], in0=cos_a[0:F, :], scalar1=cos_sin_th[0:F, 0:1], scalar2=None, op0=ALU.mult)
+        nc.vector.scalar_tensor_tensor(out=wave[0:F, :], in0=sin_a[0:F, :], scalar=cos_sin_th[0:F, 1:2], in1=cos_part[:],
+                                       op0=ALU.mult, op1=ALU.add)
 
         coefs = []
         p_cos = held.tile([P, S], F32, name="p_cos")
@@ -108,20 +98,16 @@ def tile_waveencoder_kernel(tc, x, amp, freq, offs, out):
         coefs.append(coef)
 
         for b in range(1, BLOCKS):
-            j, h = divmod(b, 2)
-            if h == 0:
-                amp_t = flip_amp(j)
             coef_psum = sums.tile([P, S], F32, name="coef_psum")
-            nc.tensor.matmul(out=coef_psum[:], lhsT=amp_t[:], rhs=wave_diag[:, h * S : (h + 1) * S], start=True, stop=True)
+            nc.tensor.matmul(out=coef_psum[:], lhsT=flip_amp(b)[:], rhs=wave[:], start=True, stop=True)
             coef = held.tile([P, S], F32, name=f"coef{b}")
             nc.scalar.copy(out=coef[:], in_=coef_psum[:])
             coefs.append(coef)
 
         for b in range(BLOCKS):
-            for half, queue in enumerate((nc.sync, nc.scalar)):
-                product = products.tile([P, 2 * S], F32, name="product")
-                for i in range(2):
-                    k = 2 * half + i
-                    picked = tables[b][:].indirect(offsets[:, k * (S // 16) : (k + 1) * (S // 16)])
-                    nc.vector.tensor_tensor(out=product[:, i * S : (i + 1) * S], in0=picked, in1=coefs[b][:], op=ALU.mult)
-                queue.dma_start(out[b * P : (b + 1) * P, 2 * half * S : 2 * (half + 1) * S], product[:])
+            for k in range(PIECES):
+                product = products.tile([P, S], F32, name="product")
+                picked = tables[b][:].indirect(offsets[:, k * (S // 16) : (k + 1) * (S // 16)])
+                nc.vector.tensor_tensor(out=product[:], in0=picked, in1=coefs[b][:], op=ALU.mult)
+                queue = nc.scalar if k % 2 == 0 else nc.sync
+                queue.dma_start(out[b * P : (b + 1) * P, k * S : (k + 1) * S], product[:])

@@ -13,6 +13,7 @@ C, S, F, N = 1024, 256, 64, 1024
 BLOCKS = C // P
 PIECES = N // S
 QUARTER = S // 4
+EARLY = 2
 
 TWO_PI = 6.283185
 TURN = 1 << 22
@@ -36,8 +37,8 @@ def tile_waveencoder_kernel(tc, x, amp, freq, offs, out):
         amp_wide = held.tile([P, BLOCKS, 2 * F], F32, name="amp_wide")
         amp_blocks = amp.rearrange("(b p) m -> p b m", p=P)
         nc.vector.memset(amp_wide[:, :, F : 2 * F], 0.0)
-        nc.scalar.dma_start(amp_wide[:, 0:1, 0:F], amp_blocks[:, 0:1, :])
-        nc.sync.dma_start(amp_wide[:, 1:BLOCKS, 0:F], amp_blocks[:, 1:BLOCKS, :])
+        nc.scalar.dma_start(amp_wide[:, 0:EARLY, 0:F], amp_blocks[:, 0:EARLY, :])
+        nc.sync.dma_start(amp_wide[:, EARLY:BLOCKS, 0:F], amp_blocks[:, EARLY:BLOCKS, :])
         tables = []
         for b in range(BLOCKS):
             table = held.tile([P, S], F32, name=f"table{b}")

@@ -105,10 +105,15 @@ def tile_waveencoder_kernel(tc, x, amp, freq, offs, out):
             nc.scalar.copy(out=coef[:], in_=coef_psum[:])
             coefs.append(coef)
 
+        stores = 0
         for b in range(BLOCKS):
-            for k in range(PIECES):
-                product = products.tile([P, S], F32, name="product")
-                picked = tables[b][:].indirect(offsets[:, k * (S // 16) : (k + 1) * (S // 16)])
-                nc.vector.tensor_tensor(out=product[:], in0=picked, in1=coefs[b][:], op=ALU.mult)
-                queue = nc.scalar if k % 2 == 0 else nc.sync
-                queue.dma_start(out[b * P : (b + 1) * P, k * S : (k + 1) * S], product[:])
+            together = 1 if b == BLOCKS - 1 else 2
+            for first in range(0, PIECES, together):
+                product = products.tile([P, together * S], F32, name="product")
+                for k in range(first, first + together):
+                    picked = tables[b][:].indirect(offsets[:, k * (S // 16) : (k + 1) * (S // 16)])
+                    nc.vector.tensor_tensor(out=product[:, (k - first) * S : (k - first + 1) * S], in0=picked,
+                                            in1=coefs[b][:], op=ALU.mult)
+                queue = nc.scalar if stores % 2 == 0 else nc.sync
+                queue.dma_start(out[b * P : (b + 1) * P, first * S : (first + together) * S], product[:])
+                stores += 1

@@ -105,7 +105,6 @@ def tile_waveencoder_kernel(tc, x, amp, freq, offs, out):
             nc.scalar.copy(out=coef[:], in_=coef_psum[:])
             coefs.append(coef)
 
-        stores = 0
         for b in range(BLOCKS):
             together = 1 if b == BLOCKS - 1 else 2
             for first in range(0, PIECES, together):
@@ -114,6 +113,4 @@ def tile_waveencoder_kernel(tc, x, amp, freq, offs, out):
                     picked = tables[b][:].indirect(offsets[:, k * (S // 16) : (k + 1) * (S // 16)])
                     nc.vector.tensor_tensor(out=product[:, (k - first) * S : (k - first + 1) * S], in0=picked,
                                             in1=coefs[b][:], op=ALU.mult)
-                queue = nc.scalar if stores % 2 == 0 else nc.sync
-                queue.dma_start(out[b * P : (b + 1) * P, first * S : (first + together) * S], product[:])
-                stores += 1
+                nc.sync.dma_start(out[b * P : (b + 1) * P, first * S : (first + together) * S], product[:])

@@ -106,11 +106,14 @@ def tile_waveencoder_kernel(tc, x, amp, freq, offs, out):
             coefs.append(coef)
 
         for b in range(BLOCKS):
-            together = 1 if b == BLOCKS - 1 else 2
-            for first in range(0, PIECES, together):
-                product = products.tile([P, together * S], F32, name="product")
-                for k in range(first, first + together):
-                    picked = tables[b][:].indirect(offsets[:, k * (S // 16) : (k + 1) * (S // 16)])
-                    nc.vector.tensor_tensor(out=product[:, (k - first) * S : (k - first + 1) * S], in0=picked,
-                                            in1=coefs[b][:], op=ALU.mult)
-                nc.sync.dma_start(out[b * P : (b + 1) * P, first * S : (first + together) * S], product[:])
+            widths = [N] if b < BLOCKS - 1 else [S, S, S, S // 2, S // 2]
+            start = 0
+            for width in widths:
+                product = products.tile([P, width], F32, name="product")
+                for j in range(start, start + width, S):
+                    n = min(S, width)
+                    picked = tables[b][:].indirect(offsets[:, j // 16 : (j + n) // 16])
+                    nc.vector.tensor_tensor(out=product[:, j - start : j - start + n], in0=picked,
+                                            in1=coefs[b][:, j % S : j % S + n], op=ALU.mult)
+                nc.sync.dma_start(out[b * P : (b + 1) * P, start : start + width], product[:])
+                start += width

@@ -29,6 +29,10 @@ def tile_waveencoder_kernel(tc, x, amp, freq, offs, out):
         tc.psum_pool(name="flipped", bufs=2) as flipped,
         tc.psum_pool(name="sums", bufs=3) as sums,
     ):
+        identity = held.tile([P, P], F32, name="identity")
+        nc.vector.memset(identity[:], 0.0)
+        make_identity(nc, identity[:], nomemset=True)
+
         freq_col = held.tile([F, 1], F32, name="freq_col")
         with nc.allow_non_contiguous_dma(reason="64 frequencies, one to a partition"):
             nc.sync.dma_start(freq_col[:], freq.rearrange("o m -> m o"))
@@ -51,9 +55,6 @@ def tile_waveencoder_kernel(tc, x, amp, freq, offs, out):
                        allow_small_or_imprecise_dtypes=True)
         nc.gpsimd.iota(position[:, S // 2 :], pattern=[[1, S // 2 + QUARTER]], base=-(S // 2), channel_multiplier=0,
                        allow_small_or_imprecise_dtypes=True)
-        identity = held.tile([P, P], F32, name="identity")
-        nc.vector.memset(identity[:], 0.0)
-        make_identity(nc, identity[:], nomemset=True)
         sine = held.tile([P, S + QUARTER], F32, name="sine")
         nc.scalar.activation(out=sine[:], in_=position[:], func=ACT.Sin, scale=TWO_PI / S)
         sin_a = sine[:, 0:S]

import concourse.mybir as mybir
from concourse.masks import make_identity

F32 = mybir.dt.float32
I32 = mybir.dt.int32
U16 = mybir.dt.uint16
U32 = mybir.dt.uint32
ALU = mybir.AluOpType
ACT = mybir.ActivationFunctionType

P = 128
C, S, F, N = 1024, 256, 64, 1024
BLOCKS = C // P
PIECES = N // S
QUARTER = S // 4
EARLY = 2

TWO_PI = 6.283185
TURN = 1 << 22

FLOPS = 2 * C * F * S + C * N


def tile_waveencoder_kernel(tc, x, amp, freq, offs, out):
    nc = tc.nc
    with (
        tc.tile_pool(name="held", bufs=1) as held,
        tc.tile_pool(name="products", bufs=8) as products,
        tc.psum_pool(name="flipped", bufs=2) as flipped,
        tc.psum_pool(name="sums", bufs=3) as sums,
    ):
        identity = held.tile([P, P], F32, name="identity")
        nc.vector.memset(identity[:], 0.0)
        make_identity(nc, identity[:], nomemset=True)

        freq_col = held.tile([F, 1], F32, name="freq_col")
        with nc.allow_non_contiguous_dma(reason="64 frequencies, one to a partition"):
            nc.sync.dma_start(freq_col[:], freq.rearrange("o m -> m o"))
        offsets = held.tile([P, N // 16], U16, name="offsets")
        nc.sync.dma_start(offsets[:], offs)
        amp_wide = held.tile([P, BLOCKS, 2 * F], F32, name="amp_wide")
        amp_blocks = amp.rearrange("(b p) m -> p b m", p=P)
        nc.vector.memset(amp_wide[:, :, F : 2 * F], 0.0)
        nc.scalar.dma_start(amp_wide[:, 0:EARLY, 0:F], amp_blocks[:, 0:EARLY, :])
        nc.sync.dma_start(amp_wide[:, EARLY:BLOCKS, 0:F], amp_blocks[:, EARLY:BLOCKS, :])
        tables = []
        for b in range(BLOCKS):
            table = held.tile([P, S], F32, name=f"table{b}")
            queue = nc.scalar if b == 0 else nc.sync
            queue.dma_start(table[:], x[b * P : (b + 1) * P, :])
            tables.append(table)

        position = held.tile([P, S + QUARTER], F32, name="position")
        nc.gpsimd.iota(position[:, 0 : S // 2], pattern=[[1, S // 2]], base=0, channel_multiplier=0,
                       allow_small_or_imprecise_dtypes=True)
        nc.gpsimd.iota(position[:, S // 2 :], pattern=[[1, S // 2 + QUARTER]], base=-(S // 2), channel_multiplier=0,
                       allow_small_or_imprecise_dtypes=True)
        sine = held.tile([P, S + QUARTER], F32, name="sine")
        nc.scalar.activation(out=sine[:], in_=position[:], func=ACT.Sin, scale=TWO_PI / S)
        sin_a = sine[:, 0:S]
        cos_a = sine[:, QUARTER : QUARTER + S]
        phase = held.tile([F, 2], F32, name="phase")
        nc.vector.memset(phase[:, 0:1], float(3 * TURN // 4))
        nc.vector.memset(phase[:, 1:2], float(TURN // 2))
        minus_half_turn = held.tile([F, 1], F32, name="minus_half_turn")
        nc.vector.memset(minus_half_turn[:], -TWO_PI / 2)
        cos_sin_th = held.tile([P, 2], F32, name="cos_sin_th")
        nc.vector.memset(cos_sin_th[F:P, :], 0.0)
        wave = held.tile([P, S], F32, name="wave")
        nc.vector.memset(wave[F:P, :], 0.0)

        turns = held.tile([F, 2], I32, name="turns")
        nc.vector.scalar_tensor_tensor(out=turns[:], in0=freq_col[:, 0:1].to_broadcast([F, 2]), scalar=float(TURN),
                                       in1=phase[:], op0=ALU.mult, op1=ALU.add)
        fraction = held.tile([F, 2], I32, name="fraction")
        nc.vector.tensor_scalar(out=fraction[:], in0=turns[:], scalar1=TURN - 1, scalar2=None, op0=ALU.bitwise_and)
        nc.scalar.activation(out=cos_sin_th[0:F, :], in_=fraction[:].bitcast(U32), func=ACT.Sin, scale=TWO_PI / TURN,
                             bias=minus_half_turn[:])

        def flip_amp(b):
            amp_t_psum = flipped.tile([P, P], F32, name="amp_t_psum")
            nc.tensor.transpose(out=amp_t_psum[:], in_=amp_wide[:, b, :], identity=identity[:])
            amp_t = held.tile([P, P], F32, name=f"amp_t{b}")
            nc.scalar.copy(out=amp_t[:], in_=amp_t_psum[:])
            return amp_t

        p_q = flipped.tile([P, 2], F32, name="p_q")
        nc.tensor.matmul(out=p_q[:], lhsT=flip_amp(0)[:], rhs=cos_sin_th[:], start=True, stop=True)

        cos_part = held.tile([F, S], F32, name="cos_part")
        nc.vector.tensor_scalar(out=cos_part[:], in0=cos_a[0:F, :], scalar1=cos_sin_th[0:F, 0:1], scalar2=None, op0=ALU.mult)
        nc.vector.scalar_tensor_tensor(out=wave[0:F, :], in0=sin_a[0:F, :], scalar=cos_sin_th[0:F, 1:2], in1=cos_part[:],
                                       op0=ALU.mult, op1=ALU.add)

        coefs = []
        p_cos = held.tile([P, S], F32, name="p_cos")
        nc.vector.tensor_scalar(out=p_cos[:], in0=cos_a, scalar1=p_q[:, 0:1], scalar2=None, op0=ALU.mult)
        coef = held.tile([P, S], F32, name="coef0")
        nc.vector.scalar_tensor_tensor(out=coef[:], in0=sin_a, scalar=p_q[:, 1:2], in1=p_cos[:], op0=ALU.mult, op1=ALU.add)
        coefs.append(coef)

        for b in range(1, BLOCKS):
            coef_psum = sums.tile([P, S], F32, name="coef_psum")
            nc.tensor.matmul(out=coef_psum[:], lhsT=flip_amp(b)[:], rhs=wave[:], start=True, stop=True)
            coef = held.tile([P, S], F32, name=f"coef{b}")
            nc.scalar.copy(out=coef[:], in_=coef_psum[:])
            coefs.append(coef)

        for b in range(BLOCKS):
            widths = [N] if b < BLOCKS - 1 else [S, S, S, S // 2, S // 2]
            start = 0
            for width in widths:
                product = products.tile([P, width], F32, name="product")
                for j in range(start, start + width, S):
                    n = min(S, width)
                    picked = tables[b][:].indirect(offsets[:, j // 16 : (j + n) // 16])
                    nc.vector.tensor_tensor(out=product[:, j - start : j - start + n], in0=picked,
                                            in1=coefs[b][:, j % S : j % S + n], op=ALU.mult)
                nc.sync.dma_start(out[b * P : (b + 1) * P, start : start + width], product[:])
                start += width
